import numpy as np
import ml_dtypes


def mxq(x, axis, fmt="e4m3"):
    dtype, down = {"e4m3": (ml_dtypes.float8_e4m3fn, 7), "e5m2": (ml_dtypes.float8_e5m2, 14)}[fmt]
    v = np.moveaxis(np.asarray(x, np.float32).astype(ml_dtypes.bfloat16).astype(np.float64), axis, -1)
    blocks = v.reshape(v.shape[:-1] + (-1, 32))
    amax = np.abs(blocks).max(-1, keepdims=True)
    byte = np.maximum(np.where(amax > 0, np.frexp(amax)[1] - 1 + 127, 0) - down, 1)
    scale = np.exp2(byte - 127.0)
    codes = (blocks / scale).astype(np.float32).astype(dtype).astype(np.float64)
    return np.moveaxis((codes * scale).reshape(v.shape), -1, axis)


WIDE = False


def mx_kscale(k):
    if not WIDE:
        return np.ones(k)
    levels = np.array([10, -10, 5, -5, 0])
    a = np.random.permutation(np.resize(levels, k // 512 * 4)).reshape(k // 512, 4)
    idx = np.arange(k)
    return np.exp2(a[idx // 512, idx % 128 // 32])


BF16 = ml_dtypes.bfloat16


def bf(x):
    return np.asarray(x, np.float32).astype(BF16)


def f64(x):
    return np.asarray(x).astype(np.float64)


E2M1 = np.array([0.0, 0.5, 1.0, 1.5, 2.0, 3.0, 4.0, 6.0, -0.0, -0.5, -1.0, -1.5, -2.0, -3.0, -4.0, -6.0])


def pack_weight(w, fmt):
    k, n = w.shape
    w = f64(bf(w)).reshape(k // 32, 32, n)
    amax = np.abs(w).max(1)
    if fmt == "e4m3":
        byte = np.frexp(amax)[1] - 1 + 127 - 7
    else:
        mant, ex = np.frexp(amax / 6.0)
        byte = np.where(mant > 0.5, ex, ex - 1) + 127
    byte = np.clip(np.where(amax > 0, byte, 1), 1, 254)
    scaled = (w * np.exp2(127.0 - byte)[:, None, :]).reshape(k, n).astype(np.float32)
    by_word = np.ascontiguousarray(scaled.reshape(k // 512, 128, 4, n).transpose(0, 1, 3, 2))
    if fmt == "e4m3":
        words = by_word.astype(ml_dtypes.float8_e4m3fn).view(np.uint8)
    else:
        c = by_word.astype(ml_dtypes.float4_e2m1fn).view(np.uint8) & 0xF
        words = c[..., 0::2] | (c[..., 1::2] << 4)
    return np.ascontiguousarray(words), np.ascontiguousarray(byte.astype(np.uint8).reshape(k // 512, 16, n))


def unpack_weight(words, scales, fmt):
    g, p, n, _ = words.shape
    if fmt == "e4m3":
        vals = np.ascontiguousarray(words).view(ml_dtypes.float8_e4m3fn).astype(np.float64)
    else:
        nib = np.empty((g, p, n, 4), np.uint8)
        nib[..., 0::2] = words & 0xF
        nib[..., 1::2] = words >> 4
        vals = E2M1[nib]
    vals = vals * np.repeat(np.exp2(scales.astype(np.float64) - 127.0), 8, axis=1)[..., None]
    return vals.transpose(0, 1, 3, 2).reshape(g * 512, n)


B, D_IN, D_OUT = 128, 2048, 2048
EPS = 0.01
FMT = "e4m3"


def setup_inputs():
    s, t = mx_kscale(D_IN), mx_kscale(D_OUT)
    x = bf(np.random.standard_normal((B, D_IN)) * s)
    W = np.random.standard_normal((D_OUT, D_IN)) / np.sqrt(D_IN) / s[None, :] * t[:, None]
    W_words, W_scales = pack_weight(np.ascontiguousarray(W.T), FMT)
    b = bf(np.random.standard_normal(D_OUT) * 0.3 * t)
    g = np.random.standard_normal((D_OUT, D_OUT)) / np.sqrt(D_OUT) / t[None, :]
    g_words, g_scales = pack_weight(np.ascontiguousarray(g.T), FMT)
    g_bias = bf(np.random.standard_normal(D_OUT) * 0.3)
    return {"x": x,
            "W_words": W_words,
            "W_scales": W_scales,
            "b": b,
            "g_words": g_words,
            "g_scales": g_scales,
            "g_bias": g_bias}


def reference(x, W_words, W_scales, b, g_words, g_scales, g_bias):
    h = (mxq(f64(x), 1, "e4m3") @ unpack_weight(W_words, W_scales, FMT)) + f64(b)
    c = np.cos((mxq(h, 1, "e4m3") @ unpack_weight(g_words, g_scales, FMT)) + f64(g_bias))
    return np.where(np.abs(c) < EPS, -c, c)

@@ -1,0 +1,219 @@
+import math
+from contextlib import ExitStack
+
+import concourse.mybir as mybir
+from concourse.masks import make_identity
+
+F32 = mybir.dt.float32
+BF16 = mybir.dt.bfloat16
+I32 = mybir.dt.int32
+U32 = mybir.dt.uint32
+U8 = mybir.dt.uint8
+FP8X4 = mybir.dt.float8_e4m3fn_x4
+ALU = mybir.AluOpType
+ACT = mybir.ActivationFunctionType
+
+P = 128
+PACK = 4
+K_PASS = P * PACK
+D = 2048
+GROUPS = D // K_PASS
+N_TILE = 512
+N_TILES = D // N_TILE
+QUADRANTS = 4
+ROWS_PER_QUADRANT = 4
+
+EPS = 0.01
+TURN = 2.0 * math.pi
+
+FLOPS = 2 * 2 * P * D * D
+
+
+def tile_onehiddenlayer_w_kernel(tc, x, W_words, W_scales, b, g_words, g_scales, g_bias, out):
+    nc = tc.nc
+    with ExitStack() as ctx:
+        ctx.enter_context(tc.manual_schedule())
+        keep = ctx.enter_context(tc.tile_pool(name="keep", bufs=1))
+        work = ctx.enter_context(tc.tile_pool(name="work", bufs=3))
+        psum_acc = ctx.enter_context(tc.psum_pool(name="psum_acc", bufs=4))
+        psum_flip = ctx.enter_context(tc.psum_pool(name="psum_flip", bufs=2))
+
+        x_rows = keep.tile([P, D], BF16)
+        weight_words = {
+            "W": keep.tile([P, GROUPS, D], U32, name="W_sb", align_bytes=64),
+            "g": keep.tile([P, GROUPS, D], U32, name="g_sb", align_bytes=64),
+        }
+        weight_planes = {
+            "W": keep.tile([P, D], U8, name="W_planes", align_bytes=64),
+            "g": keep.tile([P, D], U8, name="g_planes", align_bytes=64),
+        }
+        bias_rows = keep.tile([P, N_TILE], BF16)
+        ident_f32 = keep.tile([P, P], F32)
+        ident_bf16 = keep.tile([P, P], BF16)
+        b_sorted = keep.tile([P, GROUPS, PACK, P], BF16)
+        g_bias_turns = keep.tile([P, D], F32)
+        h_sorted = keep.tile([P, GROUPS, PACK, P], BF16)
+        grouped = {
+            "x": keep.tile([P, GROUPS, P * PACK], BF16, name="x_grouped", align_bytes=64),
+            "h": keep.tile([P, GROUPS, P * PACK], BF16, name="h_grouped", align_bytes=64),
+        }
+        codes = {
+            "x": keep.tile([P, GROUPS, P], U32, name="x_codes", align_bytes=64),
+            "h": keep.tile([P, GROUPS, P], U32, name="h_codes", align_bytes=64),
+        }
+        planes = {
+            "x": keep.tile([P, GROUPS, P], U8, name="x_planes", align_bytes=64),
+            "h": keep.tile([P, GROUPS, P], U8, name="h_planes", align_bytes=64),
+        }
+        zero_column = keep.tile([P, 1], F32)
+        sin_of_zero = keep.tile([P, 1], F32)
+
+        nc.vector.memset(bias_rows[:], 0.0)
+        nc.vector.memset(weight_planes["W"][:].bitcast(I32), 0)
+        nc.vector.memset(weight_planes["g"][:].bitcast(I32), 0)
+        nc.vector.memset(zero_column[:], 0.0)
+        make_identity(nc, ident_f32[:])
+        nc.vector.tensor_copy(out=ident_bf16[:], in_=ident_f32[:])
+        nc.scalar.activation(out=sin_of_zero[:], in_=zero_column[:], func=ACT.Sin)
+
+        def load_scales(name, scales):
+            rows = scales.bitcast(I32)
+            for q in range(QUADRANTS):
+                nc.sync.dma_start(
+                    out=weight_planes[name][32 * q : 32 * q + GROUPS * ROWS_PER_QUADRANT, :].bitcast(I32),
+                    in_=rows[:, ROWS_PER_QUADRANT * q : ROWS_PER_QUADRANT * (q + 1), :],
+                )
+
+        def load_words(name, words):
+            by_partition = words.rearrange("g p n t -> g p (n t)").bitcast(I32).rearrange("g p n -> p g n")
+            for j in range(N_TILES):
+                cols = slice(N_TILE * j, N_TILE * (j + 1))
+                nc.sync.dma_start(
+                    out=weight_words[name][:, :, cols].bitcast(I32), in_=by_partition[:, :, cols]
+                )
+
+        nc.sync.dma_start(out=x_rows[:], in_=x)
+        nc.sync.dma_start(out=bias_rows[0:N_TILES, :], in_=b.rearrange("(r c) -> r c", c=N_TILE))
+        nc.sync.dma_start(
+            out=bias_rows[N_TILES : 2 * N_TILES, :], in_=g_bias.rearrange("(r c) -> r c", c=N_TILE)
+        )
+        load_scales("W", W_scales)
+        load_words("W", W_words)
+        load_scales("g", g_scales)
+        load_words("g", g_words)
+
+        def quantise_group(name, group, flipped_by_token):
+            target = grouped[name][:, group, :]
+            if flipped_by_token.dtype == F32:
+                target = target.bitcast(F32)
+            nc.scalar.copy(
+                out=target.rearrange("p (r t) -> p r t", r=P),
+                in_=flipped_by_token,
+            )
+            nc.vector.quantize_mx(
+                out=codes[name][:, group, :].bitcast(FP8X4),
+                scales=planes[name][:, group, :],
+                in_=grouped[name][:, group, :],
+            )
+
+        def spread_bias_row(row):
+            spread = psum_acc.tile([P, N_TILE], F32, tag="acc")
+            nc.tensor.matmul(
+                out=spread[:],
+                lhsT=ident_bf16[:, row : row + 1].to_broadcast([P, P]),
+                rhs=bias_rows[:],
+                start=True,
+                stop=True,
+            )
+            return spread
+
+        def mx_product(act_name, weight_name, j):
+            cols = slice(N_TILE * j, N_TILE * (j + 1))
+            acc = psum_acc.tile([P, N_TILE], F32, tag="acc")
+            for group in range(GROUPS):
+                nc.tensor.matmul_mx(
+                    out=acc[:],
+                    lhsT=codes[act_name][:, group, :].bitcast(FP8X4),
+                    lhsT_scale=planes[act_name][:, group, :],
+                    rhs=weight_words[weight_name][:, group, cols].bitcast(FP8X4),
+                    rhs_scale=weight_planes[weight_name][ROWS_PER_QUADRANT * group : P, cols],
+                    start=(group == 0),
+                    stop=(group == GROUPS - 1),
+                )
+            return acc
+
+        x_pairs = x_rows[:].bitcast(F32)
+        PAIRS = K_PASS // 2
+        for group in range(GROUPS):
+            x_flipped = psum_flip.tile([P, 2, P], F32, tag="flipped")
+            for u in range(2):
+                nc.tensor.transpose(
+                    x_flipped[:, u, :],
+                    x_pairs[:, PAIRS * group + u : PAIRS * (group + 1) : 2],
+                    ident_f32[:],
+                )
+            quantise_group("x", group, x_flipped[:].rearrange("p u r -> p r u"))
+
+        for j in range(N_TILES):
+            spread = spread_bias_row(j)
+            nc.scalar.copy(out=b_sorted[:, j], in_=spread[:].rearrange("r (p t) -> r t p", t=PACK))
+
+        for j in range(N_TILES):
+            acc = mx_product("x", "W", j)
+            nc.vector.tensor_tensor(
+                out=h_sorted[:, j],
+                in0=acc[:].rearrange("r (p t) -> r t p", t=PACK),
+                in1=b_sorted[:, j],
+                op=ALU.add,
+            )
+            h_flipped = psum_flip.tile([P, PACK, P], BF16, tag="flipped")
+            for t in range(PACK):
+                nc.tensor.transpose(h_flipped[:, t, :], h_sorted[:, j, t, :], ident_bf16[:])
+            quantise_group("h", j, h_flipped[:].rearrange("p t r -> p r t"))
+            spread = spread_bias_row(N_TILES + j)
+            nc.scalar.activation(
+                out=g_bias_turns[:, N_TILE * j : N_TILE * (j + 1)],
+                in_=spread[:],
+                func=ACT.Copy,
+                scale=1.0 / TURN,
+                bias=0.25,
+            )
+
+        cosines = {}
+        squares = {}
+
+        def cosine_tile(j):
+            cols = slice(N_TILE * j, N_TILE * (j + 1))
+            acc = mx_product("h", "g", j)
+            turns = work.tile([P, N_TILE], F32)
+            nc.vector.scalar_tensor_tensor(
+                out=turns[:], in0=acc[:], scalar=1.0 / TURN, in1=g_bias_turns[:, cols], op0=ALU.mult, op1=ALU.add
+            )
+            whole_turns = work.tile([P, N_TILE], I32)
+            nc.vector.tensor_copy(out=whole_turns[:], in_=turns[:])
+            fraction = work.tile([P, N_TILE], F32)
+            nc.vector.tensor_tensor(out=fraction[:], in0=turns[:], in1=whole_turns[:], op=ALU.subtract)
+            cosine = work.tile([P, N_TILE], F32)
+            nc.scalar.activation(out=cosine[:], in_=fraction[:], func=ACT.Sin, scale=TURN)
+            square = work.tile([P, N_TILE], F32)
+            nc.scalar.activation(out=square[:], in_=cosine[:], func=ACT.Square)
+            cosines[j] = cosine
+            squares[j] = square
+
+        def flip_and_store(j):
+            cols = slice(N_TILE * j, N_TILE * (j + 1))
+            keep_twice = work.tile([P, N_TILE], F32)
+            nc.vector.tensor_scalar(
+                out=keep_twice[:], in0=squares[j][:], scalar1=EPS * EPS, scalar2=2.0, op0=ALU.is_ge, op1=ALU.mult
+            )
+            result = work.tile([P, N_TILE], F32)
+            nc.vector.scalar_tensor_tensor(
+                out=result[:], in0=keep_twice[:], scalar=1.0, in1=cosines[j][:], op0=ALU.subtract, op1=ALU.mult
+            )
+            nc.sync.dma_start(out=out[:, cols], in_=result[:])
+
+        for j in range(N_TILES + 1):
+            if j < N_TILES:
+                cosine_tile(j)
+            if j > 0:
+                flip_and_store(j - 1)

@@ -21,7 +21,8 @@ GROUPS = D // K_PASS
 N_TILE = 512
 N_TILES = D // N_TILE
 QUADRANTS = 4
-ROWS_PER_QUADRANT = 4
+SCALE_ROWS = 4
+LAG = 2
 
 EPS = 0.01
 TURN = 2.0 * math.pi
@@ -34,9 +35,9 @@ def tile_onehiddenlayer_w_kernel(tc, x, W_words, W_scales, b, g_words, g_scales,
     with ExitStack() as ctx:
         ctx.enter_context(tc.manual_schedule())
         keep = ctx.enter_context(tc.tile_pool(name="keep", bufs=1))
-        work = ctx.enter_context(tc.tile_pool(name="work", bufs=3))
+        work = ctx.enter_context(tc.tile_pool(name="work", bufs=LAG + 2))
         psum_acc = ctx.enter_context(tc.psum_pool(name="psum_acc", bufs=4))
-        psum_flip = ctx.enter_context(tc.psum_pool(name="psum_flip", bufs=2))
+        psum_short = ctx.enter_context(tc.psum_pool(name="psum_short", bufs=4))
 
         x_rows = keep.tile([P, D], BF16)
         weight_words = {
@@ -65,32 +66,33 @@ def tile_onehiddenlayer_w_kernel(tc, x, W_words, W_scales, b, g_words, g_scales,
             "x": keep.tile([P, GROUPS, P], U8, name="x_planes", align_bytes=64),
             "h": keep.tile([P, GROUPS, P], U8, name="h_planes", align_bytes=64),
         }
+        result = keep.tile([P, D], F32)
         zero_column = keep.tile([P, 1], F32)
         sin_of_zero = keep.tile([P, 1], F32)
+        minus_eps_squared = keep.tile([P, 1], F32)
 
         nc.vector.memset(bias_rows[:], 0.0)
         nc.vector.memset(weight_planes["W"][:].bitcast(I32), 0)
         nc.vector.memset(weight_planes["g"][:].bitcast(I32), 0)
         nc.vector.memset(zero_column[:], 0.0)
+        nc.vector.memset(minus_eps_squared[:], -EPS * EPS)
         make_identity(nc, ident_f32[:])
         nc.vector.tensor_copy(out=ident_bf16[:], in_=ident_f32[:])
         nc.scalar.activation(out=sin_of_zero[:], in_=zero_column[:], func=ACT.Sin)
+
+        out_tiles = [(N_TILE * j, N_TILE) for j in range(N_TILES - 1)]
+        out_tiles += [(D - N_TILE, N_TILE // 2), (D - N_TILE // 2, N_TILE // 2)]
 
         def load_scales(name, scales):
             rows = scales.bitcast(I32)
             for q in range(QUADRANTS):
                 nc.sync.dma_start(
-                    out=weight_planes[name][32 * q : 32 * q + GROUPS * ROWS_PER_QUADRANT, :].bitcast(I32),
-                    in_=rows[:, ROWS_PER_QUADRANT * q : ROWS_PER_QUADRANT * (q + 1), :],
+                    out=weight_planes[name][32 * q : 32 * q + GROUPS * SCALE_ROWS, :].bitcast(I32),
+                    in_=rows[:, SCALE_ROWS * q : SCALE_ROWS * (q + 1), :],
                 )
 
-        def load_words(name, words):
-            by_partition = words.rearrange("g p n t -> g p (n t)").bitcast(I32).rearrange("g p n -> p g n")
-            for j in range(N_TILES):
-                cols = slice(N_TILE * j, N_TILE * (j + 1))
-                nc.sync.dma_start(
-                    out=weight_words[name][:, :, cols].bitcast(I32), in_=by_partition[:, :, cols]
-                )
+        W_int = W_words.rearrange("g p n t -> g p (n t)").bitcast(I32)
+        g_int = g_words.rearrange("g p n t -> g p (n t)").bitcast(I32).rearrange("g p n -> p g n")
 
         nc.sync.dma_start(out=x_rows[:], in_=x)
         nc.sync.dma_start(out=bias_rows[0:N_TILES, :], in_=b.rearrange("(r c) -> r c", c=N_TILE))
@@ -98,18 +100,23 @@ def tile_onehiddenlayer_w_kernel(tc, x, W_words, W_scales, b, g_words, g_scales,
             out=bias_rows[N_TILES : 2 * N_TILES, :], in_=g_bias.rearrange("(r c) -> r c", c=N_TILE)
         )
         load_scales("W", W_scales)
-        load_words("W", W_words)
+        for group in range(GROUPS - 1):
+            nc.sync.dma_start(out=weight_words["W"][:, group, :].bitcast(I32), in_=W_int[group])
+        for j in range(N_TILES):
+            cols = slice(N_TILE * j, N_TILE * (j + 1))
+            nc.sync.dma_start(
+                out=weight_words["W"][:, GROUPS - 1, cols].bitcast(I32), in_=W_int[GROUPS - 1][:, cols]
+            )
         load_scales("g", g_scales)
-        load_words("g", g_words)
+        for first, width in out_tiles:
+            cols = slice(first, first + width)
+            nc.sync.dma_start(out=weight_words["g"][:, :, cols].bitcast(I32), in_=g_int[:, :, cols])
 
         def quantise_group(name, group, flipped_by_token):
             target = grouped[name][:, group, :]
             if flipped_by_token.dtype == F32:
                 target = target.bitcast(F32)
-            nc.scalar.copy(
-                out=target.rearrange("p (r t) -> p r t", r=P),
-                in_=flipped_by_token,
-            )
+            nc.scalar.copy(out=target.rearrange("p (r t) -> p r t", r=P), in_=flipped_by_token)
             nc.vector.quantize_mx(
                 out=codes[name][:, group, :].bitcast(FP8X4),
                 scales=planes[name][:, group, :],
@@ -117,7 +124,7 @@ def tile_onehiddenlayer_w_kernel(tc, x, W_words, W_scales, b, g_words, g_scales,
             )
 
         def spread_bias_row(row):
-            spread = psum_acc.tile([P, N_TILE], F32, tag="acc")
+            spread = psum_short.tile([P, N_TILE], F32, tag="short")
             nc.tensor.matmul(
                 out=spread[:],
                 lhsT=ident_bf16[:, row : row + 1].to_broadcast([P, P]),
@@ -127,49 +134,31 @@ def tile_onehiddenlayer_w_kernel(tc, x, W_words, W_scales, b, g_words, g_scales,
             )
             return spread
 
-        def mx_product(act_name, weight_name, j):
-            cols = slice(N_TILE * j, N_TILE * (j + 1))
-            acc = psum_acc.tile([P, N_TILE], F32, tag="acc")
-            for group in range(GROUPS):
-                nc.tensor.matmul_mx(
-                    out=acc[:],
-                    lhsT=codes[act_name][:, group, :].bitcast(FP8X4),
-                    lhsT_scale=planes[act_name][:, group, :],
-                    rhs=weight_words[weight_name][:, group, cols].bitcast(FP8X4),
-                    rhs_scale=weight_planes[weight_name][ROWS_PER_QUADRANT * group : P, cols],
-                    start=(group == 0),
-                    stop=(group == GROUPS - 1),
-                )
-            return acc
+        def mx_pass(acc, act_name, weight_name, group, cols):
+            nc.tensor.matmul_mx(
+                out=acc,
+                lhsT=codes[act_name][:, group, :].bitcast(FP8X4),
+                lhsT_scale=planes[act_name][:, group, :],
+                rhs=weight_words[weight_name][:, group, cols].bitcast(FP8X4),
+                rhs_scale=weight_planes[weight_name][SCALE_ROWS * group : P, cols],
+                start=(group == 0),
+                stop=(group == GROUPS - 1),
+            )
 
         x_pairs = x_rows[:].bitcast(F32)
-        PAIRS = K_PASS // 2
+        pairs = K_PASS // 2
         for group in range(GROUPS):
-            x_flipped = psum_flip.tile([P, 2, P], F32, tag="flipped")
+            x_flipped = psum_short.tile([P, 2, P], F32, tag="short")
             for u in range(2):
                 nc.tensor.transpose(
-                    x_flipped[:, u, :],
-                    x_pairs[:, PAIRS * group + u : PAIRS * (group + 1) : 2],
-                    ident_f32[:],
+                    x_flipped[:, u, :], x_pairs[:, pairs * group + u : pairs * (group + 1) : 2], ident_f32[:]
                 )
             quantise_group("x", group, x_flipped[:].rearrange("p u r -> p r u"))
 
         for j in range(N_TILES):
             spread = spread_bias_row(j)
             nc.scalar.copy(out=b_sorted[:, j], in_=spread[:].rearrange("r (p t) -> r t p", t=PACK))
-
         for j in range(N_TILES):
-            acc = mx_product("x", "W", j)
-            nc.vector.tensor_tensor(
-                out=h_sorted[:, j],
-                in0=acc[:].rearrange("r (p t) -> r t p", t=PACK),
-                in1=b_sorted[:, j],
-                op=ALU.add,
-            )
-            h_flipped = psum_flip.tile([P, PACK, P], BF16, tag="flipped")
-            for t in range(PACK):
-                nc.tensor.transpose(h_flipped[:, t, :], h_sorted[:, j, t, :], ident_bf16[:])
-            quantise_group("h", j, h_flipped[:].rearrange("p t r -> p r t"))
             spread = spread_bias_row(N_TILES + j)
             nc.scalar.activation(
                 out=g_bias_turns[:, N_TILE * j : N_TILE * (j + 1)],
@@ -179,41 +168,82 @@ def tile_onehiddenlayer_w_kernel(tc, x, W_words, W_scales, b, g_words, g_scales,
                 bias=0.25,
             )
 
-        cosines = {}
-        squares = {}
+        h_acc = [psum_acc.tile([P, N_TILE], F32, tag="acc", name="h_acc%d" % j) for j in range(N_TILES)]
+        for group in range(GROUPS - 1):
+            for j in range(N_TILES):
+                mx_pass(h_acc[j][:], "x", "W", group, slice(N_TILE * j, N_TILE * (j + 1)))
 
-        def cosine_tile(j):
-            cols = slice(N_TILE * j, N_TILE * (j + 1))
-            acc = mx_product("h", "g", j)
-            turns = work.tile([P, N_TILE], F32)
-            nc.vector.scalar_tensor_tensor(
-                out=turns[:], in0=acc[:], scalar=1.0 / TURN, in1=g_bias_turns[:, cols], op0=ALU.mult, op1=ALU.add
+        def close_h_tile(j):
+            mx_pass(h_acc[j][:], "x", "W", GROUPS - 1, slice(N_TILE * j, N_TILE * (j + 1)))
+            nc.vector.tensor_tensor(
+                out=h_sorted[:, j],
+                in0=h_acc[j][:].rearrange("r (p t) -> r t p", t=PACK),
+                in1=b_sorted[:, j],
+                op=ALU.add,
             )
-            whole_turns = work.tile([P, N_TILE], I32)
-            nc.vector.tensor_copy(out=whole_turns[:], in_=turns[:])
-            fraction = work.tile([P, N_TILE], F32)
-            nc.vector.tensor_tensor(out=fraction[:], in0=turns[:], in1=whole_turns[:], op=ALU.subtract)
-            cosine = work.tile([P, N_TILE], F32)
-            nc.scalar.activation(out=cosine[:], in_=fraction[:], func=ACT.Sin, scale=TURN)
-            square = work.tile([P, N_TILE], F32)
-            nc.scalar.activation(out=square[:], in_=cosine[:], func=ACT.Square)
-            cosines[j] = cosine
-            squares[j] = square
 
-        def flip_and_store(j):
-            cols = slice(N_TILE * j, N_TILE * (j + 1))
-            keep_twice = work.tile([P, N_TILE], F32)
-            nc.vector.tensor_scalar(
-                out=keep_twice[:], in0=squares[j][:], scalar1=EPS * EPS, scalar2=2.0, op0=ALU.is_ge, op1=ALU.mult
-            )
-            result = work.tile([P, N_TILE], F32)
-            nc.vector.scalar_tensor_tensor(
-                out=result[:], in0=keep_twice[:], scalar=1.0, in1=cosines[j][:], op0=ALU.subtract, op1=ALU.mult
-            )
-            nc.sync.dma_start(out=out[:, cols], in_=result[:])
+        def quantise_h_tile(j):
+            h_flipped = psum_short.tile([P, PACK, P], BF16, tag="short")
+            for t in range(PACK):
+                nc.tensor.transpose(h_flipped[:, t, :], h_sorted[:, j, t, :], ident_bf16[:])
+            quantise_group("h", j, h_flipped[:].rearrange("p t r -> p r t"))
 
         for j in range(N_TILES + 1):
             if j < N_TILES:
-                cosine_tile(j)
+                close_h_tile(j)
             if j > 0:
-                flip_and_store(j - 1)
+                quantise_h_tile(j - 1)
+
+        cosines = {}
+        signs = {}
+
+        def start_out_tile(i):
+            first, width = out_tiles[i]
+            half = width // 2
+            local = [(0, half), (half, width)]
+            acc = psum_acc.tile([P, N_TILE], F32, tag="acc")
+            for group in range(GROUPS):
+                mx_pass(acc[:, 0:width], "h", "g", group, slice(first, first + width))
+            turns = work.tile([P, N_TILE], F32)
+            whole_turns = work.tile([P, N_TILE], I32)
+            fraction = work.tile([P, N_TILE], F32)
+            cosine = work.tile([P, N_TILE], F32)
+            square = work.tile([P, N_TILE], F32)
+            sign = work.tile([P, N_TILE], F32)
+            for lo, hi in local:
+                nc.vector.scalar_tensor_tensor(
+                    out=turns[:, lo:hi],
+                    in0=acc[:, lo:hi],
+                    scalar=1.0 / TURN,
+                    in1=g_bias_turns[:, first + lo : first + hi],
+                    op0=ALU.mult,
+                    op1=ALU.add,
+                )
+            for lo, hi in local:
+                nc.vector.tensor_copy(out=whole_turns[:, lo:hi], in_=turns[:, lo:hi])
+            for lo, hi in local:
+                nc.vector.tensor_tensor(out=fraction[:, lo:hi], in0=turns[:, lo:hi], in1=whole_turns[:, lo:hi], op=ALU.subtract)
+            for lo, hi in local:
+                nc.scalar.activation(out=cosine[:, lo:hi], in_=fraction[:, lo:hi], func=ACT.Sin, scale=TURN)
+            for lo, hi in local:
+                nc.scalar.activation(out=square[:, lo:hi], in_=cosine[:, lo:hi], func=ACT.Square)
+            for lo, hi in local:
+                nc.scalar.activation(out=sign[:, lo:hi], in_=square[:, lo:hi], func=ACT.Sign, bias=minus_eps_squared[:])
+            cosines[i] = cosine
+            signs[i] = sign
+
+        def finish_out_tile(i):
+            first, width = out_tiles[i]
+            nc.vector.tensor_tensor(
+                out=result[:, first : first + width],
+                in0=cosines[i][:, 0:width],
+                in1=signs[i][:, 0:width],
+                op=ALU.mult,
+            )
+            nc.sync.dma_start(out=out[:, first : first + width], in_=result[:, first : first + width])
+
+        for i in range(len(out_tiles) + LAG):
+            if i < len(out_tiles):
+                start_out_tile(i)
+            if i >= LAG:
+                finish_out_tile(i - LAG)

@@ -91,7 +91,7 @@ def tile_onehiddenlayer_w_kernel(tc, x, W_words, W_scales, b, g_words, g_scales,
                     in_=rows[:, SCALE_ROWS * q : SCALE_ROWS * (q + 1), :],
                 )
 
-        W_int = W_words.rearrange("g p n t -> g p (n t)").bitcast(I32)
+        W_int = W_words.rearrange("g p n t -> g p (n t)").bitcast(I32).rearrange("g p n -> p g n")
         g_int = g_words.rearrange("g p n t -> g p (n t)").bitcast(I32).rearrange("g p n -> p g n")
 
         nc.sync.dma_start(out=x_rows[:], in_=x)
@@ -100,23 +100,30 @@ def tile_onehiddenlayer_w_kernel(tc, x, W_words, W_scales, b, g_words, g_scales,
             out=bias_rows[N_TILES : 2 * N_TILES, :], in_=g_bias.rearrange("(r c) -> r c", c=N_TILE)
         )
         load_scales("W", W_scales)
-        for group in range(GROUPS - 1):
-            nc.sync.dma_start(out=weight_words["W"][:, group, :].bitcast(I32), in_=W_int[group])
-        for j in range(N_TILES):
-            cols = slice(N_TILE * j, N_TILE * (j + 1))
+        W_loads = [
+            (slice(0, 2), slice(0, D // 2)),
+            (slice(2, 4), slice(0, D // 2)),
+            (slice(0, 2), slice(D // 2, D)),
+            (slice(2, 3), slice(D // 2, D)),
+            (slice(3, 4), slice(D // 2, D - N_TILE)),
+            (slice(3, 4), slice(D - N_TILE, D)),
+        ]
+        for passes, cols in W_loads:
             nc.sync.dma_start(
-                out=weight_words["W"][:, GROUPS - 1, cols].bitcast(I32), in_=W_int[GROUPS - 1][:, cols]
+                out=weight_words["W"][:, passes, cols].bitcast(I32), in_=W_int[:, passes, cols]
             )
         load_scales("g", g_scales)
         for first, width in out_tiles:
             cols = slice(first, first + width)
             nc.sync.dma_start(out=weight_words["g"][:, :, cols].bitcast(I32), in_=g_int[:, :, cols])
 
-        def quantise_group(name, group, flipped_by_token):
+        def group_by_token(name, group, flipped_by_token):
             target = grouped[name][:, group, :]
             if flipped_by_token.dtype == F32:
                 target = target.bitcast(F32)
             nc.scalar.copy(out=target.rearrange("p (r t) -> p r t", r=P), in_=flipped_by_token)
+
+        def quantise_group(name, group):
             nc.vector.quantize_mx(
                 out=codes[name][:, group, :].bitcast(FP8X4),
                 scales=planes[name][:, group, :],
@@ -153,12 +160,14 @@ def tile_onehiddenlayer_w_kernel(tc, x, W_words, W_scales, b, g_words, g_scales,
                 nc.tensor.transpose(
                     x_flipped[:, u, :], x_pairs[:, pairs * group + u : pairs * (group + 1) : 2], ident_f32[:]
                 )
-            quantise_group("x", group, x_flipped[:].rearrange("p u r -> p r u"))
+            group_by_token("x", group, x_flipped[:].rearrange("p u r -> p r u"))
+            quantise_group("x", group)
 
         for j in range(N_TILES):
             spread = spread_bias_row(j)
-            nc.scalar.copy(out=b_sorted[:, j], in_=spread[:].rearrange("r (p t) -> r t p", t=PACK))
-        for j in range(N_TILES):
+            nc.vector.tensor_copy(out=b_sorted[:, j], in_=spread[:].rearrange("r (p t) -> r t p", t=PACK))
+
+        def spread_g_bias(j):
             spread = spread_bias_row(N_TILES + j)
             nc.scalar.activation(
                 out=g_bias_turns[:, N_TILE * j : N_TILE * (j + 1)],
@@ -169,12 +178,8 @@ def tile_onehiddenlayer_w_kernel(tc, x, W_words, W_scales, b, g_words, g_scales,
             )
 
         h_acc = [psum_acc.tile([P, N_TILE], F32, tag="acc", name="h_acc%d" % j) for j in range(N_TILES)]
-        for group in range(GROUPS - 1):
-            for j in range(N_TILES):
-                mx_pass(h_acc[j][:], "x", "W", group, slice(N_TILE * j, N_TILE * (j + 1)))
 
-        def close_h_tile(j):
-            mx_pass(h_acc[j][:], "x", "W", GROUPS - 1, slice(N_TILE * j, N_TILE * (j + 1)))
+        def add_b(j):
             nc.vector.tensor_tensor(
                 out=h_sorted[:, j],
                 in0=h_acc[j][:].rearrange("r (p t) -> r t p", t=PACK),
@@ -182,17 +187,30 @@ def tile_onehiddenlayer_w_kernel(tc, x, W_words, W_scales, b, g_words, g_scales,
                 op=ALU.add,
             )
 
-        def quantise_h_tile(j):
+        def flip_h_tile(j):
             h_flipped = psum_short.tile([P, PACK, P], BF16, tag="short")
             for t in range(PACK):
                 nc.tensor.transpose(h_flipped[:, t, :], h_sorted[:, j, t, :], ident_bf16[:])
-            quantise_group("h", j, h_flipped[:].rearrange("p t r -> p r t"))
+            group_by_token("h", j, h_flipped[:].rearrange("p t r -> p r t"))
 
-        for j in range(N_TILES + 1):
-            if j < N_TILES:
-                close_h_tile(j)
-            if j > 0:
-                quantise_h_tile(j - 1)
+        for n, (passes, cols) in enumerate(W_loads):
+            for j in range(cols.start // N_TILE, cols.stop // N_TILE):
+                for group in range(passes.start, passes.stop):
+                    mx_pass(h_acc[j][:], "x", "W", group, slice(N_TILE * j, N_TILE * (j + 1)))
+                if passes.stop == GROUPS:
+                    add_b(j)
+            if n == 0:
+                for j in range(N_TILES):
+                    spread_g_bias(j)
+            if n == 1:
+                for j in range(2):
+                    flip_h_tile(j)
+                for j in range(2):
+                    quantise_group("h", j)
+        for j in range(2, N_TILES):
+            flip_h_tile(j)
+        for j in range(2, N_TILES):
+            quantise_group("h", j)
 
         cosines = {}
         signs = {}

@@ -83,11 +83,11 @@ def tile_onehiddenlayer_w_kernel(tc, x, W_words, W_scales, b, g_words, g_scales,
         out_tiles = [(N_TILE * j, N_TILE) for j in range(N_TILES - 1)]
         out_tiles += [(D - N_TILE, N_TILE // 2), (D - N_TILE // 2, N_TILE // 2)]
 
-        def load_scales(name, scales):
-            rows = scales.bitcast(I32)
+        def load_scales(name, scales, queue, word):
+            rows = scales.bitcast(word)
             for q in range(QUADRANTS):
-                nc.sync.dma_start(
-                    out=weight_planes[name][32 * q : 32 * q + GROUPS * SCALE_ROWS, :].bitcast(I32),
+                queue.dma_start(
+                    out=weight_planes[name][32 * q : 32 * q + GROUPS * SCALE_ROWS, :].bitcast(word),
                     in_=rows[:, SCALE_ROWS * q : SCALE_ROWS * (q + 1), :],
                 )
 
@@ -99,7 +99,7 @@ def tile_onehiddenlayer_w_kernel(tc, x, W_words, W_scales, b, g_words, g_scales,
         nc.sync.dma_start(
             out=bias_rows[N_TILES : 2 * N_TILES, :], in_=g_bias.rearrange("(r c) -> r c", c=N_TILE)
         )
-        load_scales("W", W_scales)
+        load_scales("W", W_scales, nc.sync, I32)
         W_loads = [
             (slice(0, 2), slice(0, D // 2)),
             (slice(2, 4), slice(0, D // 2)),
@@ -112,7 +112,7 @@ def tile_onehiddenlayer_w_kernel(tc, x, W_words, W_scales, b, g_words, g_scales,
             nc.sync.dma_start(
                 out=weight_words["W"][:, passes, cols].bitcast(I32), in_=W_int[:, passes, cols]
             )
-        load_scales("g", g_scales)
+        load_scales("g", g_scales, nc.gpsimd, F32)
         for first, width in out_tiles:
             cols = slice(first, first + width)
             nc.sync.dma_start(out=weight_words["g"][:, :, cols].bitcast(I32), in_=g_int[:, :, cols])

@@ -20,9 +20,9 @@ D = 2048
 GROUPS = D // K_PASS
 N_TILE = 512
 N_TILES = D // N_TILE
+LAST = 128
 QUADRANTS = 4
 SCALE_ROWS = 4
-LAG = 2
 
 EPS = 0.01
 TURN = 2.0 * math.pi
@@ -35,7 +35,7 @@ def tile_onehiddenlayer_w_kernel(tc, x, W_words, W_scales, b, g_words, g_scales,
     with ExitStack() as ctx:
         ctx.enter_context(tc.manual_schedule())
         keep = ctx.enter_context(tc.tile_pool(name="keep", bufs=1))
-        work = ctx.enter_context(tc.tile_pool(name="work", bufs=LAG + 2))
+        work = ctx.enter_context(tc.tile_pool(name="work", bufs=4))
         psum_acc = ctx.enter_context(tc.psum_pool(name="psum_acc", bufs=4))
         psum_short = ctx.enter_context(tc.psum_pool(name="psum_short", bufs=4))
 
@@ -81,7 +81,7 @@ def tile_onehiddenlayer_w_kernel(tc, x, W_words, W_scales, b, g_words, g_scales,
         nc.scalar.activation(out=sin_of_zero[:], in_=zero_column[:], func=ACT.Sin)
 
         out_tiles = [(N_TILE * j, N_TILE) for j in range(N_TILES - 1)]
-        out_tiles += [(D - N_TILE, N_TILE // 2), (D - N_TILE // 2, N_TILE // 2)]
+        out_tiles += [(D - N_TILE, N_TILE - LAST), (D - LAST, LAST)]
 
         def load_scales(name, scales, queue, word):
             rows = scales.bitcast(word)
@@ -100,28 +100,32 @@ def tile_onehiddenlayer_w_kernel(tc, x, W_words, W_scales, b, g_words, g_scales,
             out=bias_rows[N_TILES : 2 * N_TILES, :], in_=g_bias.rearrange("(r c) -> r c", c=N_TILE)
         )
         load_scales("W", W_scales, nc.sync, I32)
-        W_loads = [
-            (slice(0, 2), slice(0, D // 2)),
-            (slice(2, 4), slice(0, D // 2)),
-            (slice(0, 2), slice(D // 2, D)),
-            (slice(2, 3), slice(D // 2, D)),
-            (slice(3, 4), slice(D // 2, D - N_TILE)),
-            (slice(3, 4), slice(D - N_TILE, D)),
+        W_loads = [(slice(group, group + 1), slice(0, D)) for group in range(GROUPS - 1)]
+        W_loads += [
+            (slice(GROUPS - 1, GROUPS), slice(0, D // 2)),
+            (slice(GROUPS - 1, GROUPS), slice(D // 2, D - N_TILE)),
+            (slice(GROUPS - 1, GROUPS), slice(D - N_TILE, D)),
         ]
         for passes, cols in W_loads:
             nc.sync.dma_start(
                 out=weight_words["W"][:, passes, cols].bitcast(I32), in_=W_int[:, passes, cols]
             )
         load_scales("g", g_scales, nc.gpsimd, F32)
-        for first, width in out_tiles:
-            cols = slice(first, first + width)
-            nc.sync.dma_start(out=weight_words["g"][:, :, cols].bitcast(I32), in_=g_int[:, :, cols])
+        g_loads = [(slice(0, GROUPS), slice(first, first + width)) for first, width in out_tiles[:-1]]
+        g_loads += [
+            (slice(0, GROUPS - 1), slice(D - LAST, D)),
+            (slice(GROUPS - 1, GROUPS), slice(D - LAST, D)),
+        ]
+        for passes, cols in g_loads:
+            nc.sync.dma_start(
+                out=weight_words["g"][:, passes, cols].bitcast(I32), in_=g_int[:, passes, cols]
+            )
 
-        def group_by_token(name, group, flipped_by_token):
+        def group_by_token(copy, name, group, flipped_by_token):
             target = grouped[name][:, group, :]
             if flipped_by_token.dtype == F32:
                 target = target.bitcast(F32)
-            nc.scalar.copy(out=target.rearrange("p (r t) -> p r t", r=P), in_=flipped_by_token)
+            copy(out=target.rearrange("p (r t) -> p r t", r=P), in_=flipped_by_token)
 
         def quantise_group(name, group):
             nc.vector.quantize_mx(
@@ -160,7 +164,7 @@ def tile_onehiddenlayer_w_kernel(tc, x, W_words, W_scales, b, g_words, g_scales,
                 nc.tensor.transpose(
                     x_flipped[:, u, :], x_pairs[:, pairs * group + u : pairs * (group + 1) : 2], ident_f32[:]
                 )
-            group_by_token("x", group, x_flipped[:].rearrange("p u r -> p r u"))
+            group_by_token(nc.scalar.copy, "x", group, x_flipped[:].rearrange("p u r -> p r u"))
             quantise_group("x", group)
 
         for j in range(N_TILES):
@@ -187,11 +191,11 @@ def tile_onehiddenlayer_w_kernel(tc, x, W_words, W_scales, b, g_words, g_scales,
                 op=ALU.add,
             )
 
-        def flip_h_tile(j):
+        def flip_h_tile(j, copy):
             h_flipped = psum_short.tile([P, PACK, P], BF16, tag="short")
             for t in range(PACK):
                 nc.tensor.transpose(h_flipped[:, t, :], h_sorted[:, j, t, :], ident_bf16[:])
-            group_by_token("h", j, h_flipped[:].rearrange("p t r -> p r t"))
+            group_by_token(copy, "h", j, h_flipped[:].rearrange("p t r -> p r t"))
 
         for n, (passes, cols) in enumerate(W_loads):
             for j in range(cols.start // N_TILE, cols.stop // N_TILE):
@@ -202,66 +206,91 @@ def tile_onehiddenlayer_w_kernel(tc, x, W_words, W_scales, b, g_words, g_scales,
             if n == 0:
                 for j in range(N_TILES):
                     spread_g_bias(j)
-            if n == 1:
-                for j in range(2):
-                    flip_h_tile(j)
-                for j in range(2):
-                    quantise_group("h", j)
-        for j in range(2, N_TILES):
-            flip_h_tile(j)
-        for j in range(2, N_TILES):
+        for j in range(N_TILES - 1):
+            flip_h_tile(j, nc.scalar.copy)
+        for j in range(N_TILES - 2):
+            quantise_group("h", j)
+        flip_h_tile(N_TILES - 1, nc.vector.tensor_copy)
+        for j in range(N_TILES - 2, N_TILES):
             quantise_group("h", j)
 
         cosines = {}
         signs = {}
 
+        def multiply_out_tile(i):
+            first, width = out_tiles[i]
+            acc = psum_acc.tile([P, N_TILE], F32, tag="acc")
+            pieces = [(0, width)] if width != N_TILE - LAST else [(0, N_TILE // 2), (N_TILE // 2, width)]
+            for lo, hi in pieces:
+                for group in range(GROUPS):
+                    mx_pass(acc[:, lo:hi], "h", "g", group, slice(first + lo, first + hi))
+            return acc
+
+        def to_turns(acc, first, lo, hi, target):
+            nc.vector.scalar_tensor_tensor(
+                out=target[:, lo:hi],
+                in0=acc[:, lo:hi],
+                scalar=1.0 / TURN,
+                in1=g_bias_turns[:, first + lo : first + hi],
+                op0=ALU.mult,
+                op1=ALU.add,
+            )
+
         def start_out_tile(i):
             first, width = out_tiles[i]
-            half = width // 2
-            local = [(0, half), (half, width)]
-            acc = psum_acc.tile([P, N_TILE], F32, tag="acc")
-            for group in range(GROUPS):
-                mx_pass(acc[:, 0:width], "h", "g", group, slice(first, first + width))
+            acc = multiply_out_tile(i)
             turns = work.tile([P, N_TILE], F32)
             whole_turns = work.tile([P, N_TILE], I32)
             fraction = work.tile([P, N_TILE], F32)
             cosine = work.tile([P, N_TILE], F32)
             square = work.tile([P, N_TILE], F32)
             sign = work.tile([P, N_TILE], F32)
+            cosines[i] = cosine
+            signs[i] = sign
+            if width > LAST:
+                local = [(0, width // 2), (width // 2, width)]
+                for lo, hi in local:
+                    to_turns(acc, first, lo, hi, turns)
+                for lo, hi in local:
+                    nc.vector.tensor_copy(out=whole_turns[:, lo:hi], in_=turns[:, lo:hi])
+            else:
+                local = [(0, width)]
+                to_turns(acc, first, 0, width, turns)
+                to_turns(acc, first, 0, width, whole_turns)
+                flip_sign(i - 2, 0, N_TILE // 2)
             for lo, hi in local:
-                nc.vector.scalar_tensor_tensor(
-                    out=turns[:, lo:hi],
-                    in0=acc[:, lo:hi],
-                    scalar=1.0 / TURN,
-                    in1=g_bias_turns[:, first + lo : first + hi],
-                    op0=ALU.mult,
-                    op1=ALU.add,
+                nc.vector.tensor_tensor(
+                    out=fraction[:, lo:hi], in0=turns[:, lo:hi], in1=whole_turns[:, lo:hi], op=ALU.subtract
                 )
-            for lo, hi in local:
-                nc.vector.tensor_copy(out=whole_turns[:, lo:hi], in_=turns[:, lo:hi])
-            for lo, hi in local:
-                nc.vector.tensor_tensor(out=fraction[:, lo:hi], in0=turns[:, lo:hi], in1=whole_turns[:, lo:hi], op=ALU.subtract)
             for lo, hi in local:
                 nc.scalar.activation(out=cosine[:, lo:hi], in_=fraction[:, lo:hi], func=ACT.Sin, scale=TURN)
             for lo, hi in local:
                 nc.scalar.activation(out=square[:, lo:hi], in_=cosine[:, lo:hi], func=ACT.Square)
             for lo, hi in local:
                 nc.scalar.activation(out=sign[:, lo:hi], in_=square[:, lo:hi], func=ACT.Sign, bias=minus_eps_squared[:])
-            cosines[i] = cosine
-            signs[i] = sign
 
-        def finish_out_tile(i):
+        def flip_sign(i, lo, hi):
             first, width = out_tiles[i]
             nc.vector.tensor_tensor(
-                out=result[:, first : first + width],
-                in0=cosines[i][:, 0:width],
-                in1=signs[i][:, 0:width],
+                out=result[:, first + lo : first + hi],
+                in0=cosines[i][:, lo:hi],
+                in1=signs[i][:, lo:hi],
                 op=ALU.mult,
             )
+
+        def store(i):
+            first, width = out_tiles[i]
             nc.sync.dma_start(out=out[:, first : first + width], in_=result[:, first : first + width])
 
-        for i in range(len(out_tiles) + LAG):
-            if i < len(out_tiles):
-                start_out_tile(i)
-            if i >= LAG:
-                finish_out_tile(i - LAG)
+        start_out_tile(0)
+        for i in (1, 2):
+            start_out_tile(i)
+            flip_sign(i - 1, 0, N_TILE)
+            store(i - 1)
+        start_out_tile(3)
+        start_out_tile(4)
+        flip_sign(2, N_TILE // 2, N_TILE)
+        store(2)
+        for i in (3, 4):
+            flip_sign(i, 0, out_tiles[i][1])
+            store(i)

@@ -20,7 +20,8 @@ D = 2048
 GROUPS = D // K_PASS
 N_TILE = 512
 N_TILES = D // N_TILE
-LAST = 128
+OUT_WIDTHS = (512, 512, 384, 384, 256)
+NO_SIGN_TILE = 3
 QUADRANTS = 4
 SCALE_ROWS = 4
 
@@ -35,7 +36,7 @@ def tile_onehiddenlayer_w_kernel(tc, x, W_words, W_scales, b, g_words, g_scales,
     with ExitStack() as ctx:
         ctx.enter_context(tc.manual_schedule())
         keep = ctx.enter_context(tc.tile_pool(name="keep", bufs=1))
-        work = ctx.enter_context(tc.tile_pool(name="work", bufs=4))
+        work = ctx.enter_context(tc.tile_pool(name="work", bufs=5))
         psum_acc = ctx.enter_context(tc.psum_pool(name="psum_acc", bufs=4))
         psum_short = ctx.enter_context(tc.psum_pool(name="psum_short", bufs=4))
 
@@ -80,8 +81,10 @@ def tile_onehiddenlayer_w_kernel(tc, x, W_words, W_scales, b, g_words, g_scales,
         nc.vector.tensor_copy(out=ident_bf16[:], in_=ident_f32[:])
         nc.scalar.activation(out=sin_of_zero[:], in_=zero_column[:], func=ACT.Sin)
 
-        out_tiles = [(N_TILE * j, N_TILE) for j in range(N_TILES - 1)]
-        out_tiles += [(D - N_TILE, N_TILE - LAST), (D - LAST, LAST)]
+        out_tiles = []
+        for width in OUT_WIDTHS:
+            out_tiles.append((sum(w for f, w in out_tiles), width))
+        last_cols = slice(D - OUT_WIDTHS[-1], D)
 
         def load_scales(name, scales, queue, word):
             rows = scales.bitcast(word)
@@ -113,8 +116,8 @@ def tile_onehiddenlayer_w_kernel(tc, x, W_words, W_scales, b, g_words, g_scales,
         load_scales("g", g_scales, nc.gpsimd, F32)
         g_loads = [(slice(0, GROUPS), slice(first, first + width)) for first, width in out_tiles[:-1]]
         g_loads += [
-            (slice(0, GROUPS - 1), slice(D - LAST, D)),
-            (slice(GROUPS - 1, GROUPS), slice(D - LAST, D)),
+            (slice(0, GROUPS - 1), last_cols),
+            (slice(GROUPS - 1, GROUPS), last_cols),
         ]
         for passes, cols in g_loads:
             nc.sync.dma_start(
@@ -216,11 +219,12 @@ def tile_onehiddenlayer_w_kernel(tc, x, W_words, W_scales, b, g_words, g_scales,
 
         cosines = {}
         signs = {}
+        squares = {}
 
         def multiply_out_tile(i):
             first, width = out_tiles[i]
             acc = psum_acc.tile([P, N_TILE], F32, tag="acc")
-            pieces = [(0, width)] if width != N_TILE - LAST else [(0, N_TILE // 2), (N_TILE // 2, width)]
+            pieces = [(0, width)] if width != 384 else [(0, 256), (256, width)]
             for lo, hi in pieces:
                 for group in range(GROUPS):
                     mx_pass(acc[:, lo:hi], "h", "g", group, slice(first + lo, first + hi))
@@ -247,17 +251,11 @@ def tile_onehiddenlayer_w_kernel(tc, x, W_words, W_scales, b, g_words, g_scales,
             sign = work.tile([P, N_TILE], F32)
             cosines[i] = cosine
             signs[i] = sign
-            if width > LAST:
-                local = [(0, width // 2), (width // 2, width)]
-                for lo, hi in local:
-                    to_turns(acc, first, lo, hi, turns)
-                for lo, hi in local:
-                    nc.vector.tensor_copy(out=whole_turns[:, lo:hi], in_=turns[:, lo:hi])
-            else:
-                local = [(0, width)]
-                to_turns(acc, first, 0, width, turns)
-                to_turns(acc, first, 0, width, whole_turns)
-                flip_sign(i - 2, 0, N_TILE // 2)
+            local = [(0, width // 2), (width // 2, width)]
+            for lo, hi in local:
+                to_turns(acc, first, lo, hi, turns)
+            for lo, hi in local:
+                nc.vector.tensor_copy(out=whole_turns[:, lo:hi], in_=turns[:, lo:hi])
             for lo, hi in local:
                 nc.vector.tensor_tensor(
                     out=fraction[:, lo:hi], in0=turns[:, lo:hi], in1=whole_turns[:, lo:hi], op=ALU.subtract
@@ -266,31 +264,45 @@ def tile_onehiddenlayer_w_kernel(tc, x, W_words, W_scales, b, g_words, g_scales,
                 nc.scalar.activation(out=cosine[:, lo:hi], in_=fraction[:, lo:hi], func=ACT.Sin, scale=TURN)
             for lo, hi in local:
                 nc.scalar.activation(out=square[:, lo:hi], in_=cosine[:, lo:hi], func=ACT.Square)
-            for lo, hi in local:
-                nc.scalar.activation(out=sign[:, lo:hi], in_=square[:, lo:hi], func=ACT.Sign, bias=minus_eps_squared[:])
+            if i != NO_SIGN_TILE:
+                for lo, hi in local:
+                    nc.scalar.activation(out=sign[:, lo:hi], in_=square[:, lo:hi], func=ACT.Sign, bias=minus_eps_squared[:])
+            squares[i] = square
 
-        def flip_sign(i, lo, hi):
+        def finish_out_tile(i):
             first, width = out_tiles[i]
-            nc.vector.tensor_tensor(
-                out=result[:, first + lo : first + hi],
-                in0=cosines[i][:, lo:hi],
-                in1=signs[i][:, lo:hi],
-                op=ALU.mult,
-            )
-
-        def store(i):
-            first, width = out_tiles[i]
+            if i == NO_SIGN_TILE:
+                nc.vector.scalar_tensor_tensor(
+                    out=result[:, first : first + width],
+                    in0=signs[i][:, 0:width],
+                    scalar=1.0,
+                    in1=cosines[i][:, 0:width],
+                    op0=ALU.subtract,
+                    op1=ALU.mult,
+                )
+            else:
+                nc.vector.tensor_tensor(
+                    out=result[:, first : first + width],
+                    in0=cosines[i][:, 0:width],
+                    in1=signs[i][:, 0:width],
+                    op=ALU.mult,
+                )
             nc.sync.dma_start(out=out[:, first : first + width], in_=result[:, first : first + width])
 
         start_out_tile(0)
-        for i in (1, 2):
+        start_out_tile(1)
+        finish_out_tile(0)
+        for i in range(2, len(out_tiles)):
             start_out_tile(i)
-            flip_sign(i - 1, 0, N_TILE)
-            store(i - 1)
-        start_out_tile(3)
-        start_out_tile(4)
-        flip_sign(2, N_TILE // 2, N_TILE)
-        store(2)
-        for i in (3, 4):
-            flip_sign(i, 0, out_tiles[i][1])
-            store(i)
+        finish_out_tile(1)
+        width = OUT_WIDTHS[NO_SIGN_TILE]
+        nc.vector.tensor_scalar(
+            out=signs[NO_SIGN_TILE][:, 0:width],
+            in0=squares[NO_SIGN_TILE][:, 0:width],
+            scalar1=EPS * EPS,
+            scalar2=2.0,
+            op0=ALU.is_ge,
+            op1=ALU.mult,
+        )
+        for i in range(2, len(out_tiles)):
+            finish_out_tile(i)

@@ -72,8 +72,8 @@ def tile_onehiddenlayer_w_kernel(tc, x, W_words, W_scales, b, g_words, g_scales,
         sin_of_zero = keep.tile([P, 1], F32)
         minus_eps_squared = keep.tile([P, 1], F32)
 
-        nc.vector.memset(bias_rows[:], 0.0)
         nc.vector.memset(weight_planes["W"][:].bitcast(I32), 0)
+        nc.vector.memset(bias_rows[:], 0.0)
         nc.vector.memset(weight_planes["g"][:].bitcast(I32), 0)
         nc.vector.memset(zero_column[:], 0.0)
         nc.vector.memset(minus_eps_squared[:], -EPS * EPS)
@@ -86,11 +86,11 @@ def tile_onehiddenlayer_w_kernel(tc, x, W_words, W_scales, b, g_words, g_scales,
             out_tiles.append((sum(w for f, w in out_tiles), width))
         last_cols = slice(D - OUT_WIDTHS[-1], D)
 
-        def load_scales(name, scales, queue, word):
-            rows = scales.bitcast(word)
+        def load_scales(name, scales):
+            rows = scales.bitcast(F32)
             for q in range(QUADRANTS):
-                queue.dma_start(
-                    out=weight_planes[name][32 * q : 32 * q + GROUPS * SCALE_ROWS, :].bitcast(word),
+                nc.gpsimd.dma_start(
+                    out=weight_planes[name][32 * q : 32 * q + GROUPS * SCALE_ROWS, :].bitcast(F32),
                     in_=rows[:, SCALE_ROWS * q : SCALE_ROWS * (q + 1), :],
                 )
 
@@ -102,7 +102,10 @@ def tile_onehiddenlayer_w_kernel(tc, x, W_words, W_scales, b, g_words, g_scales,
         nc.sync.dma_start(
             out=bias_rows[N_TILES : 2 * N_TILES, :], in_=g_bias.rearrange("(r c) -> r c", c=N_TILE)
         )
-        load_scales("W", W_scales, nc.sync, I32)
+        load_scales("W", W_scales)
+        nc.gpsimd.memset(weight_words["W"][:, 2, 0:16], 0)
+        load_scales("g", g_scales)
+        nc.gpsimd.memset(weight_words["g"][:, 0, out_tiles[1][0] : out_tiles[1][0] + 16], 0)
         W_loads = [(slice(group, group + 1), slice(0, D)) for group in range(GROUPS - 1)]
         W_loads += [
             (slice(GROUPS - 1, GROUPS), slice(0, D // 2)),
@@ -113,7 +116,6 @@ def tile_onehiddenlayer_w_kernel(tc, x, W_words, W_scales, b, g_words, g_scales,
             nc.sync.dma_start(
                 out=weight_words["W"][:, passes, cols].bitcast(I32), in_=W_int[:, passes, cols]
             )
-        load_scales("g", g_scales, nc.gpsimd, F32)
         g_loads = [(slice(0, GROUPS), slice(first, first + width)) for first, width in out_tiles[:-1]]
         g_loads += [
             (slice(0, GROUPS - 1), last_cols),
@@ -174,7 +176,7 @@ def tile_onehiddenlayer_w_kernel(tc, x, W_words, W_scales, b, g_words, g_scales,
             spread = spread_bias_row(j)
             nc.vector.tensor_copy(out=b_sorted[:, j], in_=spread[:].rearrange("r (p t) -> r t p", t=PACK))
 
-        def spread_g_bias(j):
+        for j in range(N_TILES):
             spread = spread_bias_row(N_TILES + j)
             nc.scalar.activation(
                 out=g_bias_turns[:, N_TILE * j : N_TILE * (j + 1)],
@@ -206,9 +208,6 @@ def tile_onehiddenlayer_w_kernel(tc, x, W_words, W_scales, b, g_words, g_scales,
                     mx_pass(h_acc[j][:], "x", "W", group, slice(N_TILE * j, N_TILE * (j + 1)))
                 if passes.stop == GROUPS:
                     add_b(j)
-            if n == 0:
-                for j in range(N_TILES):
-                    spread_g_bias(j)
         for j in range(N_TILES - 1):
             flip_h_tile(j, nc.scalar.copy)
         for j in range(N_TILES - 2):

@@ -52,9 +52,9 @@ def tile_onehiddenlayer_w_kernel(tc, x, W_words, W_scales, b, g_words, g_scales,
         bias_rows = keep.tile([P, N_TILE], BF16)
         ident_f32 = keep.tile([P, P], F32)
         ident_bf16 = keep.tile([P, P], BF16)
-        b_sorted = keep.tile([P, GROUPS, PACK, P], BF16)
+        b_sorted = keep.tile([P, GROUPS, 2, P, 2], BF16)
         g_bias_turns = keep.tile([P, D], F32)
-        h_sorted = keep.tile([P, GROUPS, PACK, P], BF16)
+        h_sorted = keep.tile([P, GROUPS, 2, P, 2], BF16)
         grouped = {
             "x": keep.tile([P, GROUPS, P * PACK], BF16, name="x_grouped", align_bytes=64),
             "h": keep.tile([P, GROUPS, P * PACK], BF16, name="h_grouped", align_bytes=64),
@@ -174,7 +174,7 @@ def tile_onehiddenlayer_w_kernel(tc, x, W_words, W_scales, b, g_words, g_scales,
 
         for j in range(N_TILES):
             spread = spread_bias_row(j)
-            nc.vector.tensor_copy(out=b_sorted[:, j], in_=spread[:].rearrange("r (p t) -> r t p", t=PACK))
+            nc.vector.tensor_copy(out=b_sorted[:, j], in_=spread[:].rearrange("r (p u e) -> r u p e", u=2, e=2))
 
         for j in range(N_TILES):
             spread = spread_bias_row(N_TILES + j)
@@ -191,16 +191,17 @@ def tile_onehiddenlayer_w_kernel(tc, x, W_words, W_scales, b, g_words, g_scales,
         def add_b(j):
             nc.vector.tensor_tensor(
                 out=h_sorted[:, j],
-                in0=h_acc[j][:].rearrange("r (p t) -> r t p", t=PACK),
+                in0=h_acc[j][:].rearrange("r (p u e) -> r u p e", u=2, e=2),
                 in1=b_sorted[:, j],
                 op=ALU.add,
             )
 
         def flip_h_tile(j, copy):
-            h_flipped = psum_short.tile([P, PACK, P], BF16, tag="short")
-            for t in range(PACK):
-                nc.tensor.transpose(h_flipped[:, t, :], h_sorted[:, j, t, :], ident_bf16[:])
-            group_by_token(copy, "h", j, h_flipped[:].rearrange("p t r -> p r t"))
+            h_pairs = h_sorted[:, j].rearrange("r u p e -> r (u p e)").bitcast(F32)
+            h_flipped = psum_short.tile([P, 2, P], F32, tag="short")
+            for u in range(2):
+                nc.tensor.transpose(h_flipped[:, u, :], h_pairs[:, P * u : P * (u + 1)], ident_f32[:])
+            group_by_token(copy, "h", j, h_flipped[:].rearrange("p u r -> p r u"))
 
         for n, (passes, cols) in enumerate(W_loads):
             for j in range(cols.start // N_TILE, cols.stop // N_TILE):
@@ -254,7 +255,10 @@ def tile_onehiddenlayer_w_kernel(tc, x, W_words, W_scales, b, g_words, g_scales,
             for lo, hi in local:
                 to_turns(acc, first, lo, hi, turns)
             for lo, hi in local:
-                nc.vector.tensor_copy(out=whole_turns[:, lo:hi], in_=turns[:, lo:hi])
+                if i == len(out_tiles) - 1:
+                    to_turns(acc, first, lo, hi, whole_turns)
+                else:
+                    nc.vector.tensor_copy(out=whole_turns[:, lo:hi], in_=turns[:, lo:hi])
             for lo, hi in local:
                 nc.vector.tensor_tensor(
                     out=fraction[:, lo:hi], in0=turns[:, lo:hi], in1=whole_turns[:, lo:hi], op=ALU.subtract
@@ -288,12 +292,10 @@ def tile_onehiddenlayer_w_kernel(tc, x, W_words, W_scales, b, g_words, g_scales,
                 )
             nc.sync.dma_start(out=out[:, first : first + width], in_=result[:, first : first + width])
 
-        start_out_tile(0)
-        start_out_tile(1)
-        finish_out_tile(0)
-        for i in range(2, len(out_tiles)):
+        for i in range(len(out_tiles)):
             start_out_tile(i)
-        finish_out_tile(1)
+            if i in (1, 2):
+                finish_out_tile(i - 1)
         width = OUT_WIDTHS[NO_SIGN_TILE]
         nc.vector.tensor_scalar(
             out=signs[NO_SIGN_TILE][:, 0:width],

@@ -272,25 +272,26 @@ def tile_onehiddenlayer_w_kernel(tc, x, W_words, W_scales, b, g_words, g_scales,
                     nc.scalar.activation(out=sign[:, lo:hi], in_=square[:, lo:hi], func=ACT.Sign, bias=minus_eps_squared[:])
             squares[i] = square
 
-        def finish_out_tile(i):
+        def finish_out_tile(i, pieces=1):
             first, width = out_tiles[i]
-            if i == NO_SIGN_TILE:
-                nc.vector.scalar_tensor_tensor(
-                    out=result[:, first : first + width],
-                    in0=signs[i][:, 0:width],
-                    scalar=1.0,
-                    in1=cosines[i][:, 0:width],
-                    op0=ALU.subtract,
-                    op1=ALU.mult,
-                )
-            else:
-                nc.vector.tensor_tensor(
-                    out=result[:, first : first + width],
-                    in0=cosines[i][:, 0:width],
-                    in1=signs[i][:, 0:width],
-                    op=ALU.mult,
-                )
-            nc.sync.dma_start(out=out[:, first : first + width], in_=result[:, first : first + width])
+            step = width // pieces
+            for lo in range(0, width, step):
+                cols = slice(first + lo, first + lo + step)
+                local = slice(lo, lo + step)
+                if i == NO_SIGN_TILE:
+                    nc.vector.scalar_tensor_tensor(
+                        out=result[:, cols],
+                        in0=signs[i][:, local],
+                        scalar=1.0,
+                        in1=cosines[i][:, local],
+                        op0=ALU.subtract,
+                        op1=ALU.mult,
+                    )
+                else:
+                    nc.vector.tensor_tensor(
+                        out=result[:, cols], in0=cosines[i][:, local], in1=signs[i][:, local], op=ALU.mult
+                    )
+                nc.sync.dma_start(out=out[:, cols], in_=result[:, cols])
 
         for i in range(len(out_tiles)):
             start_out_tile(i)
@@ -305,5 +306,6 @@ def tile_onehiddenlayer_w_kernel(tc, x, W_words, W_scales, b, g_words, g_scales,
             op0=ALU.is_ge,
             op1=ALU.mult,
         )
-        for i in range(2, len(out_tiles)):
+        for i in range(2, len(out_tiles) - 1):
             finish_out_tile(i)
+        finish_out_tile(len(out_tiles) - 1, pieces=2)

import math
from contextlib import ExitStack

import concourse.mybir as mybir
from concourse.masks import make_identity

F32 = mybir.dt.float32
BF16 = mybir.dt.bfloat16
I32 = mybir.dt.int32
U32 = mybir.dt.uint32
U8 = mybir.dt.uint8
FP8X4 = mybir.dt.float8_e4m3fn_x4
ALU = mybir.AluOpType
ACT = mybir.ActivationFunctionType

P = 128
PACK = 4
K_PASS = P * PACK
D = 2048
GROUPS = D // K_PASS
N_TILE = 512
N_TILES = D // N_TILE
OUT_WIDTHS = (512, 512, 384, 384, 256)
NO_SIGN_TILE = 3
QUADRANTS = 4
SCALE_ROWS = 4

EPS = 0.01
TURN = 2.0 * math.pi

FLOPS = 2 * 2 * P * D * D


def tile_onehiddenlayer_w_kernel(tc, x, W_words, W_scales, b, g_words, g_scales, g_bias, out):
    nc = tc.nc
    with ExitStack() as ctx:
        ctx.enter_context(tc.manual_schedule())
        keep = ctx.enter_context(tc.tile_pool(name="keep", bufs=1))
        work = ctx.enter_context(tc.tile_pool(name="work", bufs=5))
        psum_acc = ctx.enter_context(tc.psum_pool(name="psum_acc", bufs=4))
        psum_short = ctx.enter_context(tc.psum_pool(name="psum_short", bufs=4))

        x_rows = keep.tile([P, D], BF16)
        weight_words = {
            "W": keep.tile([P, GROUPS, D], U32, name="W_sb", align_bytes=64),
            "g": keep.tile([P, GROUPS, D], U32, name="g_sb", align_bytes=64),
        }
        weight_planes = {
            "W": keep.tile([P, D], U8, name="W_planes", align_bytes=64),
            "g": keep.tile([P, D], U8, name="g_planes", align_bytes=64),
        }
        bias_rows = keep.tile([P, N_TILE], BF16)
        ident_f32 = keep.tile([P, P], F32)
        ident_bf16 = keep.tile([P, P], BF16)
        b_sorted = keep.tile([P, GROUPS, 2, P, 2], BF16)
        g_bias_turns = keep.tile([P, D], F32)
        h_sorted = keep.tile([P, GROUPS, 2, P, 2], BF16)
        grouped = {
            "x": keep.tile([P, GROUPS, P * PACK], BF16, name="x_grouped", align_bytes=64),
            "h": keep.tile([P, GROUPS, P * PACK], BF16, name="h_grouped", align_bytes=64),
        }
        codes = {
            "x": keep.tile([P, GROUPS, P], U32, name="x_codes", align_bytes=64),
            "h": keep.tile([P, GROUPS, P], U32, name="h_codes", align_bytes=64),
        }
        planes = {
            "x": keep.tile([P, GROUPS, P], U8, name="x_planes", align_bytes=64),
            "h": keep.tile([P, GROUPS, P], U8, name="h_planes", align_bytes=64),
        }
        result = keep.tile([P, D], F32)
        zero_column = keep.tile([P, 1], F32)
        sin_of_zero = keep.tile([P, 1], F32)
        minus_eps_squared = keep.tile([P, 1], F32)

        nc.vector.memset(weight_planes["W"][:].bitcast(I32), 0)
        nc.vector.memset(bias_rows[:], 0.0)
        nc.vector.memset(weight_planes["g"][:].bitcast(I32), 0)
        nc.vector.memset(zero_column[:], 0.0)
        nc.vector.memset(minus_eps_squared[:], -EPS * EPS)
        make_identity(nc, ident_f32[:])
        nc.vector.tensor_copy(out=ident_bf16[:], in_=ident_f32[:])
        nc.scalar.activation(out=sin_of_zero[:], in_=zero_column[:], func=ACT.Sin)

        out_tiles = []
        for width in OUT_WIDTHS:
            out_tiles.append((sum(w for f, w in out_tiles), width))
        last_cols = slice(D - OUT_WIDTHS[-1], D)

        def load_scales(name, scales):
            rows = scales.bitcast(F32)
            for q in range(QUADRANTS):
                nc.gpsimd.dma_start(
                    out=weight_planes[name][32 * q : 32 * q + GROUPS * SCALE_ROWS, :].bitcast(F32),
                    in_=rows[:, SCALE_ROWS * q : SCALE_ROWS * (q + 1), :],
                )

        W_int = W_words.rearrange("g p n t -> g p (n t)").bitcast(I32).rearrange("g p n -> p g n")
        g_int = g_words.rearrange("g p n t -> g p (n t)").bitcast(I32).rearrange("g p n -> p g n")

        nc.sync.dma_start(out=x_rows[:], in_=x)
        nc.sync.dma_start(out=bias_rows[0:N_TILES, :], in_=b.rearrange("(r c) -> r c", c=N_TILE))
        nc.sync.dma_start(
            out=bias_rows[N_TILES : 2 * N_TILES, :], in_=g_bias.rearrange("(r c) -> r c", c=N_TILE)
        )
        load_scales("W", W_scales)
        nc.gpsimd.memset(weight_words["W"][:, 2, 0:16], 0)
        load_scales("g", g_scales)
        nc.gpsimd.memset(weight_words["g"][:, 0, out_tiles[1][0] : out_tiles[1][0] + 16], 0)
        W_loads = [(slice(group, group + 1), slice(0, D)) for group in range(GROUPS - 1)]
        W_loads += [
            (slice(GROUPS - 1, GROUPS), slice(0, D // 2)),
            (slice(GROUPS - 1, GROUPS), slice(D // 2, D - N_TILE)),
            (slice(GROUPS - 1, GROUPS), slice(D - N_TILE, D)),
        ]
        for passes, cols in W_loads:
            nc.sync.dma_start(
                out=weight_words["W"][:, passes, cols].bitcast(I32), in_=W_int[:, passes, cols]
            )
        g_loads = [(slice(0, GROUPS), slice(first, first + width)) for first, width in out_tiles[:-1]]
        g_loads += [
            (slice(0, GROUPS - 1), last_cols),
            (slice(GROUPS - 1, GROUPS), last_cols),
        ]
        for passes, cols in g_loads:
            nc.sync.dma_start(
                out=weight_words["g"][:, passes, cols].bitcast(I32), in_=g_int[:, passes, cols]
            )

        def group_by_token(copy, name, group, flipped_by_token):
            target = grouped[name][:, group, :]
            if flipped_by_token.dtype == F32:
                target = target.bitcast(F32)
            copy(out=target.rearrange("p (r t) -> p r t", r=P), in_=flipped_by_token)

        def quantise_group(name, group):
            nc.vector.quantize_mx(
                out=codes[name][:, group, :].bitcast(FP8X4),
                scales=planes[name][:, group, :],
                in_=grouped[name][:, group, :],
            )

        def spread_bias_row(row):
            spread = psum_short.tile([P, N_TILE], F32, tag="short")
            nc.tensor.matmul(
                out=spread[:],
                lhsT=ident_bf16[:, row : row + 1].to_broadcast([P, P]),
                rhs=bias_rows[:],
                start=True,
                stop=True,
            )
            return spread

        def mx_pass(acc, act_name, weight_name, group, cols):
            nc.tensor.matmul_mx(
                out=acc,
                lhsT=codes[act_name][:, group, :].bitcast(FP8X4),
                lhsT_scale=planes[act_name][:, group, :],
                rhs=weight_words[weight_name][:, group, cols].bitcast(FP8X4),
                rhs_scale=weight_planes[weight_name][SCALE_ROWS * group : P, cols],
                start=(group == 0),
                stop=(group == GROUPS - 1),
            )

        x_pairs = x_rows[:].bitcast(F32)
        pairs = K_PASS // 2
        for group in range(GROUPS):
            x_flipped = psum_short.tile([P, 2, P], F32, tag="short")
            for u in range(2):
                nc.tensor.transpose(
                    x_flipped[:, u, :], x_pairs[:, pairs * group + u : pairs * (group + 1) : 2], ident_f32[:]
                )
            group_by_token(nc.scalar.copy, "x", group, x_flipped[:].rearrange("p u r -> p r u"))
            quantise_group("x", group)

        for j in range(N_TILES):
            spread = spread_bias_row(j)
            nc.vector.tensor_copy(out=b_sorted[:, j], in_=spread[:].rearrange("r (p u e) -> r u p e", u=2, e=2))

        for j in range(N_TILES):
            spread = spread_bias_row(N_TILES + j)
            nc.scalar.activation(
                out=g_bias_turns[:, N_TILE * j : N_TILE * (j + 1)],
                in_=spread[:],
                func=ACT.Copy,
                scale=1.0 / TURN,
                bias=0.25,
            )

        h_acc = [psum_acc.tile([P, N_TILE], F32, tag="acc", name="h_acc%d" % j) for j in range(N_TILES)]

        def add_b(j):
            nc.vector.tensor_tensor(
                out=h_sorted[:, j],
                in0=h_acc[j][:].rearrange("r (p u e) -> r u p e", u=2, e=2),
                in1=b_sorted[:, j],
                op=ALU.add,
            )

        def flip_h_tile(j, copy):
            h_pairs = h_sorted[:, j].rearrange("r u p e -> r (u p e)").bitcast(F32)
            h_flipped = psum_short.tile([P, 2, P], F32, tag="short")
            for u in range(2):
                nc.tensor.transpose(h_flipped[:, u, :], h_pairs[:, P * u : P * (u + 1)], ident_f32[:])
            group_by_token(copy, "h", j, h_flipped[:].rearrange("p u r -> p r u"))

        for n, (passes, cols) in enumerate(W_loads):
            for j in range(cols.start // N_TILE, cols.stop // N_TILE):
                for group in range(passes.start, passes.stop):
                    mx_pass(h_acc[j][:], "x", "W", group, slice(N_TILE * j, N_TILE * (j + 1)))
                if passes.stop == GROUPS:
                    add_b(j)
        for j in range(N_TILES - 1):
            flip_h_tile(j, nc.scalar.copy)
        for j in range(N_TILES - 2):
            quantise_group("h", j)
        flip_h_tile(N_TILES - 1, nc.vector.tensor_copy)
        for j in range(N_TILES - 2, N_TILES):
            quantise_group("h", j)

        cosines = {}
        signs = {}
        squares = {}

        def multiply_out_tile(i):
            first, width = out_tiles[i]
            acc = psum_acc.tile([P, N_TILE], F32, tag="acc")
            pieces = [(0, width)] if width != 384 else [(0, 256), (256, width)]
            for lo, hi in pieces:
                for group in range(GROUPS):
                    mx_pass(acc[:, lo:hi], "h", "g", group, slice(first + lo, first + hi))
            return acc

        def to_turns(acc, first, lo, hi, target):
            nc.vector.scalar_tensor_tensor(
                out=target[:, lo:hi],
                in0=acc[:, lo:hi],
                scalar=1.0 / TURN,
                in1=g_bias_turns[:, first + lo : first + hi],
                op0=ALU.mult,
                op1=ALU.add,
            )

        def start_out_tile(i):
            first, width = out_tiles[i]
            acc = multiply_out_tile(i)
            turns = work.tile([P, N_TILE], F32)
            whole_turns = work.tile([P, N_TILE], I32)
            fraction = work.tile([P, N_TILE], F32)
            cosine = work.tile([P, N_TILE], F32)
            square = work.tile([P, N_TILE], F32)
            sign = work.tile([P, N_TILE], F32)
            cosines[i] = cosine
            signs[i] = sign
            local = [(0, width // 2), (width // 2, width)]
            for lo, hi in local:
                to_turns(acc, first, lo, hi, turns)
            for lo, hi in local:
                if i == len(out_tiles) - 1:
                    to_turns(acc, first, lo, hi, whole_turns)
                else:
                    nc.vector.tensor_copy(out=whole_turns[:, lo:hi], in_=turns[:, lo:hi])
            for lo, hi in local:
                nc.vector.tensor_tensor(
                    out=fraction[:, lo:hi], in0=turns[:, lo:hi], in1=whole_turns[:, lo:hi], op=ALU.subtract
                )
            for lo, hi in local:
                nc.scalar.activation(out=cosine[:, lo:hi], in_=fraction[:, lo:hi], func=ACT.Sin, scale=TURN)
            for lo, hi in local:
                nc.scalar.activation(out=square[:, lo:hi], in_=cosine[:, lo:hi], func=ACT.Square)
            if i != NO_SIGN_TILE:
                for lo, hi in local:
                    nc.scalar.activation(out=sign[:, lo:hi], in_=square[:, lo:hi], func=ACT.Sign, bias=minus_eps_squared[:])
            squares[i] = square

        def finish_out_tile(i, pieces=1):
            first, width = out_tiles[i]
            step = width // pieces
            for lo in range(0, width, step):
                cols = slice(first + lo, first + lo + step)
                local = slice(lo, lo + step)
                if i == NO_SIGN_TILE:
                    nc.vector.scalar_tensor_tensor(
                        out=result[:, cols],
                        in0=signs[i][:, local],
                        scalar=1.0,
                        in1=cosines[i][:, local],
                        op0=ALU.subtract,
                        op1=ALU.mult,
                    )
                else:
                    nc.vector.tensor_tensor(
                        out=result[:, cols], in0=cosines[i][:, local], in1=signs[i][:, local], op=ALU.mult
                    )
                nc.sync.dma_start(out=out[:, cols], in_=result[:, cols])

        for i in range(len(out_tiles)):
            start_out_tile(i)
            if i in (1, 2):
                finish_out_tile(i - 1)
        width = OUT_WIDTHS[NO_SIGN_TILE]
        nc.vector.tensor_scalar(
            out=signs[NO_SIGN_TILE][:, 0:width],
            in0=squares[NO_SIGN_TILE][:, 0:width],
            scalar1=EPS * EPS,
            scalar2=2.0,
            op0=ALU.is_ge,
            op1=ALU.mult,
        )
        for i in range(2, len(out_tiles) - 1):
            finish_out_tile(i)
        finish_out_tile(len(out_tiles) - 1, pieces=2)
